import numpy as np
import ml_dtypes

BF16 = ml_dtypes.bfloat16


def bf(x):
    return np.asarray(x, np.float32).astype(BF16)


def f32(x):
    return np.asarray(x, np.float32)


def f64(x):
    return np.asarray(x).astype(np.float64)


def striped(idx):
    return np.tile(idx.reshape(-1, 16).T, (8, 1))


D, S, M, N = 128, 1024, 512, 1024


def setup_inputs():
    return {"q": bf(np.random.standard_normal((D, S))), "k": bf(np.random.standard_normal((D, M))), "v": bf(2.0 * np.random.standard_normal((M, D))), "offs": striped(np.random.permutation(S)[:N])}


def reference(q, k, v, offs):
    idx = offs[:16].T.reshape(-1)
    logits = (f64(k).T @ f64(q)[:, idx]) / np.sqrt(D)
    e = np.exp(logits)
    return (f64(v).T @ e) / e.sum(axis=0, keepdims=True)

@@ -1,0 +1,110 @@
+import math
+
+import concourse.mybir as mybir
+from concourse.masks import make_identity
+
+BF16, F32, U16 = mybir.dt.bfloat16, mybir.dt.float32, mybir.dt.uint16
+EXP = mybir.ActivationFunctionType.Exp
+X = mybir.AxisListType.X
+
+P = 128
+TOKENS = 1024
+KEYS = 512
+N = 1024
+PIECE = 512
+PIECES = N // PIECE
+KEY_BLOCKS = KEYS // P
+QUERY_BLOCKS = PIECE // P
+ONES = P
+VALUE_COLUMNS = 144
+
+FLOPS = 2 * (2 * P * KEYS * N)
+
+
+def tile_longcontextattention_kernel(tc, q, k, v, offs, out):
+    nc = tc.nc
+    with (
+        tc.tile_pool(name="held", bufs=1) as held,
+        tc.tile_pool(name="work", bufs=2) as work,
+        tc.psum_pool(name="product_banks", bufs=4) as product_banks,
+        tc.psum_pool(name="wide_banks", bufs=2) as wide_banks,
+        tc.psum_pool(name="sums_banks", bufs=2) as sums_banks,
+    ):
+        offsets = held.tile([P, N // 16], U16, name="offsets")
+        nc.sync.dma_start(offsets[:], offs)
+        queries = held.tile([P, TOKENS], BF16, name="queries")
+        nc.scalar.dma_start(queries[:], q)
+        keys = held.tile([P, KEYS], BF16, name="keys")
+        nc.sync.dma_start(keys[:], k)
+
+        warm = held.tile([P, 1], F32, name="warm")
+        nc.vector.memset(warm[:], 0.0)
+        nc.scalar.activation(warm[:], warm[:], EXP)
+
+        values = held.tile([P, KEY_BLOCKS, VALUE_COLUMNS], BF16, name="values")
+        nc.gpsimd.dma_start(values[:, :, 0:P], v.rearrange("(b p) d -> p b d", p=P))
+        nc.vector.memset(values[:, :, ONES:VALUE_COLUMNS], 1.0)
+
+        identity = held.tile([P, P], F32, name="identity")
+        make_identity(nc, identity[:])
+        all_ones = held.tile([P, P], BF16, name="all_ones")
+        nc.vector.memset(all_ones[:], 1.0)
+
+        logits = [[] for piece in range(PIECES)]
+        largest = [held.tile([P, PIECE], F32, name=f"largest_{piece}") for piece in range(PIECES)]
+        for b in range(KEY_BLOCKS):
+            for piece in range(PIECES):
+                piece_offsets = offsets[:, piece * (PIECE // 16) : (piece + 1) * (PIECE // 16)]
+                product = product_banks.tile([P, PIECE], F32, name="product")
+                nc.tensor.matmul(
+                    product[:], keys[:, b * P : (b + 1) * P], queries[:].indirect(piece_offsets), start=True, stop=True
+                )
+                logits[piece].append(held.tile([P, PIECE], F32, name=f"logits_{piece}_{b}"))
+                nc.scalar.copy(logits[piece][b][:], product[:])
+                if b > 0:
+                    so_far = logits[piece][0] if b == 1 else largest[piece]
+                    nc.vector.tensor_max(largest[piece][:], product[:], so_far[:])
+
+        tops = []
+        for piece in range(PIECES):
+            flipped_largest = wide_banks.tile([P, QUERY_BLOCKS, P], F32, name="flipped_largest", tag="wide")
+            for c in range(QUERY_BLOCKS):
+                nc.tensor.transpose(flipped_largest[:, c, :], largest[piece][:, c * P : (c + 1) * P], identity[:])
+            top = work.tile([P, QUERY_BLOCKS], F32, name="top")
+            nc.vector.reduce_max(top[:], flipped_largest[:], X)
+            diagonals = work.tile([P, QUERY_BLOCKS, P], BF16, name="diagonals")
+            for c in range(QUERY_BLOCKS):
+                nc.vector.tensor_scalar_mul(diagonals[:, c, :], identity[:], top[:, c : c + 1])
+            tops.append(wide_banks.tile([P, PIECE], F32, name=f"tops_{piece}", tag="wide"))
+            nc.tensor.matmul(
+                tops[piece][:], all_ones[:], diagonals[:].rearrange("p c i -> p (c i)"), start=True, stop=True
+            )
+
+        weights = []
+        for piece in range(PIECES):
+            weights.append([])
+            for b in range(KEY_BLOCKS):
+                nc.vector.tensor_sub(logits[piece][b][:], logits[piece][b][:], tops[piece][:])
+                weights[piece].append(held.tile([P, PIECE], BF16, name=f"e_{piece}_{b}"))
+                nc.scalar.activation(weights[piece][b][:], logits[piece][b][:], EXP, scale=1.0 / math.sqrt(P))
+
+        for piece in range(PIECES):
+            flipped = wide_banks.tile([P, PIECE], F32, name="flipped", tag="wide")
+            for c in range(QUERY_BLOCKS):
+                sums = sums_banks.tile([P, P + 1], F32, name="sums")
+                for b in range(KEY_BLOCKS):
+                    nc.tensor.matmul(
+                        sums[:],
+                        weights[piece][b][:, c * P : (c + 1) * P],
+                        values[:, b, 0 : P + 1],
+                        start=(b == 0),
+                        stop=(b == KEY_BLOCKS - 1),
+                    )
+                inverse = work.tile([P, 1], F32, name="inverse")
+                nc.vector.reciprocal(inverse[:], sums[:, ONES : ONES + 1])
+                attended = work.tile([P, P], F32, name="attended")
+                nc.vector.tensor_scalar_mul(attended[:], sums[:, 0:P], inverse[:])
+                nc.tensor.transpose(flipped[:, c * P : (c + 1) * P], attended[:], identity[:])
+            result = work.tile([P, PIECE], F32, name="result")
+            nc.vector.tensor_copy(result[:], flipped[:])
+            nc.sync.dma_start(out[:, piece * PIECE : (piece + 1) * PIECE], result[:])

@@ -5,6 +5,7 @@ from concourse.masks import make_identity
 
 BF16, F32, U16 = mybir.dt.bfloat16, mybir.dt.float32, mybir.dt.uint16
 EXP = mybir.ActivationFunctionType.Exp
+COPY = mybir.ActivationFunctionType.Copy
 X = mybir.AxisListType.X
 
 P = 128
@@ -17,6 +18,7 @@ KEY_BLOCKS = KEYS // P
 QUERY_BLOCKS = PIECE // P
 ONES = P
 VALUE_COLUMNS = 144
+WARM_UPS = 4
 
 FLOPS = 2 * (2 * P * KEYS * N)
 
@@ -26,9 +28,7 @@ def tile_longcontextattention_kernel(tc, q, k, v, offs, out):
     with (
         tc.tile_pool(name="held", bufs=1) as held,
         tc.tile_pool(name="work", bufs=2) as work,
-        tc.psum_pool(name="product_banks", bufs=4) as product_banks,
-        tc.psum_pool(name="wide_banks", bufs=2) as wide_banks,
-        tc.psum_pool(name="sums_banks", bufs=2) as sums_banks,
+        tc.psum_pool(name="banks", bufs=8) as banks,
     ):
         offsets = held.tile([P, N // 16], U16, name="offsets")
         nc.sync.dma_start(offsets[:], offs)
@@ -47,38 +47,43 @@ def tile_longcontextattention_kernel(tc, q, k, v, offs, out):
 
         identity = held.tile([P, P], F32, name="identity")
         make_identity(nc, identity[:])
-        all_ones = held.tile([P, P], BF16, name="all_ones")
-        nc.vector.memset(all_ones[:], 1.0)
+        identity_bf16 = held.tile([P, P], BF16, name="identity_bf16")
+        make_identity(nc, identity_bf16[:])
+
+        zeros = held.tile([P, PIECE], BF16, name="zeros")
+        nc.vector.memset(zeros[:], 0.0)
+        for i in range(WARM_UPS):
+            unused = banks.tile([P, PIECE], F32, name="unused", tag="bank")
+            nc.tensor.matmul(unused[:], zeros[:, 0:P], zeros[:], start=True, stop=True)
 
         logits = [[] for piece in range(PIECES)]
-        largest = [held.tile([P, PIECE], F32, name=f"largest_{piece}") for piece in range(PIECES)]
-        for b in range(KEY_BLOCKS):
-            for piece in range(PIECES):
+        largest = [held.tile([P, PIECE], BF16, name=f"largest_{piece}") for piece in range(PIECES)]
+        for piece in range(PIECES):
+            for b in range(KEY_BLOCKS):
                 piece_offsets = offsets[:, piece * (PIECE // 16) : (piece + 1) * (PIECE // 16)]
-                product = product_banks.tile([P, PIECE], F32, name="product")
+                product = banks.tile([P, PIECE], F32, name="product", tag="bank")
                 nc.tensor.matmul(
                     product[:], keys[:, b * P : (b + 1) * P], queries[:].indirect(piece_offsets), start=True, stop=True
                 )
-                logits[piece].append(held.tile([P, PIECE], F32, name=f"logits_{piece}_{b}"))
-                nc.scalar.copy(logits[piece][b][:], product[:])
                 if b > 0:
                     so_far = logits[piece][0] if b == 1 else largest[piece]
                     nc.vector.tensor_max(largest[piece][:], product[:], so_far[:])
+                logits[piece].append(held.tile([P, PIECE], F32, name=f"logits_{piece}_{b}"))
+                nc.scalar.copy(logits[piece][b][:], product[:])
 
         tops = []
         for piece in range(PIECES):
-            flipped_largest = wide_banks.tile([P, QUERY_BLOCKS, P], F32, name="flipped_largest", tag="wide")
+            flipped_largest = banks.tile([P, QUERY_BLOCKS, P], BF16, name="flipped_largest", tag="bank")
             for c in range(QUERY_BLOCKS):
-                nc.tensor.transpose(flipped_largest[:, c, :], largest[piece][:, c * P : (c + 1) * P], identity[:])
-            top = work.tile([P, QUERY_BLOCKS], F32, name="top")
-            nc.vector.reduce_max(top[:], flipped_largest[:], X)
-            diagonals = work.tile([P, QUERY_BLOCKS, P], BF16, name="diagonals")
+                nc.tensor.transpose(flipped_largest[:, c, :], largest[piece][:, c * P : (c + 1) * P], identity_bf16[:])
+            top = work.tile([P, QUERY_BLOCKS], BF16, name="top")
+            with nc.allow_low_precision(reason="the maximum of bfloat16 numbers is one of them"):
+                nc.vector.reduce_max(top[:], flipped_largest[:], X)
+            tops.append(banks.tile([P, PIECE], BF16, name=f"tops_{piece}", tag="bank"))
             for c in range(QUERY_BLOCKS):
-                nc.vector.tensor_scalar_mul(diagonals[:, c, :], identity[:], top[:, c : c + 1])
-            tops.append(wide_banks.tile([P, PIECE], F32, name=f"tops_{piece}", tag="wide"))
-            nc.tensor.matmul(
-                tops[piece][:], all_ones[:], diagonals[:].rearrange("p c i -> p (c i)"), start=True, stop=True
-            )
+                nc.tensor.transpose(
+                    tops[piece][:, c * P : (c + 1) * P], top[:, c : c + 1].to_broadcast([P, P]), identity_bf16[:]
+                )
 
         weights = []
         for piece in range(PIECES):
@@ -89,22 +94,29 @@ def tile_longcontextattention_kernel(tc, q, k, v, offs, out):
                 nc.scalar.activation(weights[piece][b][:], logits[piece][b][:], EXP, scale=1.0 / math.sqrt(P))
 
         for piece in range(PIECES):
-            flipped = wide_banks.tile([P, PIECE], F32, name="flipped", tag="wide")
-            for c in range(QUERY_BLOCKS):
-                sums = sums_banks.tile([P, P + 1], F32, name="sums")
-                for b in range(KEY_BLOCKS):
+            sums = [banks.tile([P, P + 1], F32, name=f"sums_{c}", tag="bank") for c in range(QUERY_BLOCKS)]
+            for b in range(KEY_BLOCKS):
+                for c in range(QUERY_BLOCKS):
                     nc.tensor.matmul(
-                        sums[:],
+                        sums[c][:],
                         weights[piece][b][:, c * P : (c + 1) * P],
                         values[:, b, 0 : P + 1],
                         start=(b == 0),
                         stop=(b == KEY_BLOCKS - 1),
                     )
-                inverse = work.tile([P, 1], F32, name="inverse")
-                nc.vector.reciprocal(inverse[:], sums[:, ONES : ONES + 1])
-                attended = work.tile([P, P], F32, name="attended")
-                nc.vector.tensor_scalar_mul(attended[:], sums[:, 0:P], inverse[:])
-                nc.tensor.transpose(flipped[:, c * P : (c + 1) * P], attended[:], identity[:])
+            flipped = banks.tile([P, PIECE], F32, name="flipped", tag="bank")
             result = work.tile([P, PIECE], F32, name="result")
-            nc.vector.tensor_copy(result[:], flipped[:])
-            nc.sync.dma_start(out[:, piece * PIECE : (piece + 1) * PIECE], result[:])
+            for c in range(QUERY_BLOCKS):
+                inverse = work.tile([P, 1], F32, name="inverse")
+                nc.vector.reciprocal(inverse[:], sums[c][:, ONES : ONES + 1])
+                attended = work.tile([P, P], F32, name="attended")
+                if c % 2 == 0:
+                    nc.vector.tensor_scalar_mul(attended[:], sums[c][:, 0:P], inverse[:])
+                else:
+                    nc.scalar.activation(attended[:], sums[c][:, 0:P], COPY, scale=inverse[:])
+                nc.tensor.transpose(flipped[:, c * P : (c + 1) * P], attended[:], identity[:])
+            half = PIECE // 2
+            for h, queue in enumerate((nc.sync, nc.scalar)):
+                columns = slice(h * half, (h + 1) * half)
+                nc.vector.tensor_copy(result[:, columns], flipped[:, columns])
+                queue.dma_start(out[:, piece * PIECE + h * half : piece * PIECE + (h + 1) * half], result[:, columns])

@@ -18,7 +18,6 @@ KEY_BLOCKS = KEYS // P
 QUERY_BLOCKS = PIECE // P
 ONES = P
 VALUE_COLUMNS = 144
-WARM_UPS = 4
 
 FLOPS = 2 * (2 * P * KEYS * N)
 
@@ -49,12 +48,6 @@ def tile_longcontextattention_kernel(tc, q, k, v, offs, out):
         make_identity(nc, identity[:])
         identity_bf16 = held.tile([P, P], BF16, name="identity_bf16")
         make_identity(nc, identity_bf16[:])
-
-        zeros = held.tile([P, PIECE], BF16, name="zeros")
-        nc.vector.memset(zeros[:], 0.0)
-        for i in range(WARM_UPS):
-            unused = banks.tile([P, PIECE], F32, name="unused", tag="bank")
-            nc.tensor.matmul(unused[:], zeros[:, 0:P], zeros[:], start=True, stop=True)
 
         logits = [[] for piece in range(PIECES)]
         largest = [held.tile([P, PIECE], BF16, name=f"largest_{piece}") for piece in range(PIECES)]

@@ -18,6 +18,7 @@ KEY_BLOCKS = KEYS // P
 QUERY_BLOCKS = PIECE // P
 ONES = P
 VALUE_COLUMNS = 144
+WARM_UPS = 4
 
 FLOPS = 2 * (2 * P * KEYS * N)
 
@@ -49,6 +50,12 @@ def tile_longcontextattention_kernel(tc, q, k, v, offs, out):
         identity_bf16 = held.tile([P, P], BF16, name="identity_bf16")
         make_identity(nc, identity_bf16[:])
 
+        zeros = held.tile([P, PIECE], BF16, name="zeros")
+        nc.vector.memset(zeros[:], 0.0)
+        for i in range(WARM_UPS):
+            unused = banks.tile([P, PIECE], F32, name="unused", tag="bank")
+            nc.tensor.matmul(unused[:], zeros[:, 0:P], zeros[:], start=True, stop=True)
+
         logits = [[] for piece in range(PIECES)]
         largest = [held.tile([P, PIECE], BF16, name=f"largest_{piece}") for piece in range(PIECES)]
         for piece in range(PIECES):
@@ -64,18 +71,21 @@ def tile_longcontextattention_kernel(tc, q, k, v, offs, out):
                 logits[piece].append(held.tile([P, PIECE], F32, name=f"logits_{piece}_{b}"))
                 nc.scalar.copy(logits[piece][b][:], product[:])
 
-        tops = []
+        top = []
         for piece in range(PIECES):
             flipped_largest = banks.tile([P, QUERY_BLOCKS, P], BF16, name="flipped_largest", tag="bank")
             for c in range(QUERY_BLOCKS):
                 nc.tensor.transpose(flipped_largest[:, c, :], largest[piece][:, c * P : (c + 1) * P], identity_bf16[:])
-            top = work.tile([P, QUERY_BLOCKS], BF16, name="top")
+            top.append(held.tile([P, QUERY_BLOCKS], BF16, name=f"top_{piece}"))
             with nc.allow_low_precision(reason="the maximum of bfloat16 numbers is one of them"):
-                nc.vector.reduce_max(top[:], flipped_largest[:], X)
+                nc.vector.reduce_max(top[piece][:], flipped_largest[:], X)
+
+        tops = []
+        for piece in range(PIECES):
             tops.append(banks.tile([P, PIECE], BF16, name=f"tops_{piece}", tag="bank"))
             for c in range(QUERY_BLOCKS):
                 nc.tensor.transpose(
-                    tops[piece][:, c * P : (c + 1) * P], top[:, c : c + 1].to_broadcast([P, P]), identity_bf16[:]
+                    tops[piece][:, c * P : (c + 1) * P], top[piece][:, c : c + 1].to_broadcast([P, P]), identity_bf16[:]
                 )
 
         weights = []
@@ -86,30 +96,36 @@ def tile_longcontextattention_kernel(tc, q, k, v, offs, out):
                 weights[piece].append(held.tile([P, PIECE], BF16, name=f"e_{piece}_{b}"))
                 nc.scalar.activation(weights[piece][b][:], logits[piece][b][:], EXP, scale=1.0 / math.sqrt(P))
 
+        sums = []
         for piece in range(PIECES):
-            sums = [banks.tile([P, P + 1], F32, name=f"sums_{c}", tag="bank") for c in range(QUERY_BLOCKS)]
+            sums.append([banks.tile([P, P + 1], F32, name=f"sums_{piece}_{c}", tag="bank") for c in range(QUERY_BLOCKS)])
             for b in range(KEY_BLOCKS):
                 for c in range(QUERY_BLOCKS):
                     nc.tensor.matmul(
-                        sums[c][:],
+                        sums[piece][c][:],
                         weights[piece][b][:, c * P : (c + 1) * P],
                         values[:, b, 0 : P + 1],
                         start=(b == 0),
                         stop=(b == KEY_BLOCKS - 1),
                     )
-            flipped = banks.tile([P, PIECE], F32, name="flipped", tag="bank")
-            result = work.tile([P, PIECE], F32, name="result")
+
+        flipped = []
+        for piece in range(PIECES):
+            flipped.append(banks.tile([P, PIECE], F32, name=f"flipped_{piece}", tag="bank"))
             for c in range(QUERY_BLOCKS):
                 inverse = work.tile([P, 1], F32, name="inverse")
-                nc.vector.reciprocal(inverse[:], sums[c][:, ONES : ONES + 1])
+                nc.vector.reciprocal(inverse[:], sums[piece][c][:, ONES : ONES + 1])
                 attended = work.tile([P, P], F32, name="attended")
                 if c % 2 == 0:
-                    nc.vector.tensor_scalar_mul(attended[:], sums[c][:, 0:P], inverse[:])
+                    nc.vector.tensor_scalar_mul(attended[:], sums[piece][c][:, 0:P], inverse[:])
                 else:
-                    nc.scalar.activation(attended[:], sums[c][:, 0:P], COPY, scale=inverse[:])
-                nc.tensor.transpose(flipped[:, c * P : (c + 1) * P], attended[:], identity[:])
-            half = PIECE // 2
+                    nc.scalar.activation(attended[:], sums[piece][c][:, 0:P], COPY, scale=inverse[:])
+                nc.tensor.transpose(flipped[piece][:, c * P : (c + 1) * P], attended[:], identity[:])
+
+        half = PIECE // 2
+        for piece in range(PIECES):
+            result = work.tile([P, PIECE], F32, name="result")
             for h, queue in enumerate((nc.sync, nc.scalar)):
                 columns = slice(h * half, (h + 1) * half)
-                nc.vector.tensor_copy(result[:, columns], flipped[:, columns])
+                nc.vector.tensor_copy(result[:, columns], flipped[piece][:, columns])
                 queue.dma_start(out[:, piece * PIECE + h * half : piece * PIECE + (h + 1) * half], result[:, columns])

@@ -16,6 +16,7 @@ PIECE = 512
 PIECES = N // PIECE
 KEY_BLOCKS = KEYS // P
 QUERY_BLOCKS = PIECE // P
+HALF = PIECE // 2
 ONES = P
 VALUE_COLUMNS = 144
 WARM_UPS = 4
@@ -59,8 +60,8 @@ def tile_longcontextattention_kernel(tc, q, k, v, offs, out):
         logits = [[] for piece in range(PIECES)]
         largest = [held.tile([P, PIECE], BF16, name=f"largest_{piece}") for piece in range(PIECES)]
         for piece in range(PIECES):
+            piece_offsets = offsets[:, piece * (PIECE // 16) : (piece + 1) * (PIECE // 16)]
             for b in range(KEY_BLOCKS):
-                piece_offsets = offsets[:, piece * (PIECE // 16) : (piece + 1) * (PIECE // 16)]
                 product = banks.tile([P, PIECE], F32, name="product", tag="bank")
                 nc.tensor.matmul(
                     product[:], keys[:, b * P : (b + 1) * P], queries[:].indirect(piece_offsets), start=True, stop=True
@@ -88,13 +89,13 @@ def tile_longcontextattention_kernel(tc, q, k, v, offs, out):
                     tops[piece][:, c * P : (c + 1) * P], top[piece][:, c : c + 1].to_broadcast([P, P]), identity_bf16[:]
                 )
 
-        weights = []
+        e = [[] for piece in range(PIECES)]
         for piece in range(PIECES):
-            weights.append([])
             for b in range(KEY_BLOCKS):
-                nc.vector.tensor_sub(logits[piece][b][:], logits[piece][b][:], tops[piece][:])
-                weights[piece].append(held.tile([P, PIECE], BF16, name=f"e_{piece}_{b}"))
-                nc.scalar.activation(weights[piece][b][:], logits[piece][b][:], EXP, scale=1.0 / math.sqrt(P))
+                shifted = held.tile([P, PIECE], F32, name=f"shifted_{piece}_{b}")
+                nc.vector.tensor_sub(shifted[:], logits[piece][b][:], tops[piece][:])
+                e[piece].append(held.tile([P, PIECE], BF16, name=f"e_{piece}_{b}"))
+                nc.scalar.activation(e[piece][b][:], shifted[:], EXP, scale=1.0 / math.sqrt(P))
 
         sums = []
         for piece in range(PIECES):
@@ -103,7 +104,7 @@ def tile_longcontextattention_kernel(tc, q, k, v, offs, out):
                 for c in range(QUERY_BLOCKS):
                     nc.tensor.matmul(
                         sums[piece][c][:],
-                        weights[piece][b][:, c * P : (c + 1) * P],
+                        e[piece][b][:, c * P : (c + 1) * P],
                         values[:, b, 0 : P + 1],
                         start=(b == 0),
                         stop=(b == KEY_BLOCKS - 1),
@@ -111,21 +112,23 @@ def tile_longcontextattention_kernel(tc, q, k, v, offs, out):
 
         flipped = []
         for piece in range(PIECES):
-            flipped.append(banks.tile([P, PIECE], F32, name=f"flipped_{piece}", tag="bank"))
+            inverse = work.tile([P, QUERY_BLOCKS], F32, name="inverse")
             for c in range(QUERY_BLOCKS):
-                inverse = work.tile([P, 1], F32, name="inverse")
-                nc.vector.reciprocal(inverse[:], sums[piece][c][:, ONES : ONES + 1])
+                nc.vector.reciprocal(inverse[:, c : c + 1], sums[piece][c][:, ONES : ONES + 1])
+            flipped.append([banks.tile([P, HALF], F32, name=f"flipped_{piece}_{h}", tag="bank") for h in range(2)])
+            for c in range(QUERY_BLOCKS):
                 attended = work.tile([P, P], F32, name="attended")
                 if c % 2 == 0:
-                    nc.vector.tensor_scalar_mul(attended[:], sums[piece][c][:, 0:P], inverse[:])
+                    nc.vector.tensor_scalar_mul(attended[:], sums[piece][c][:, 0:P], inverse[:, c : c + 1])
                 else:
-                    nc.scalar.activation(attended[:], sums[piece][c][:, 0:P], COPY, scale=inverse[:])
-                nc.tensor.transpose(flipped[piece][:, c * P : (c + 1) * P], attended[:], identity[:])
+                    nc.scalar.activation(attended[:], sums[piece][c][:, 0:P], COPY, scale=inverse[:, c : c + 1])
+                h, place = divmod(c * P, HALF)
+                nc.tensor.transpose(flipped[piece][h][:, place : place + P], attended[:], identity[:])
 
-        half = PIECE // 2
         for piece in range(PIECES):
-            result = work.tile([P, PIECE], F32, name="result")
-            for h, queue in enumerate((nc.sync, nc.scalar)):
-                columns = slice(h * half, (h + 1) * half)
-                nc.vector.tensor_copy(result[:, columns], flipped[piece][:, columns])
-                queue.dma_start(out[:, piece * PIECE + h * half : piece * PIECE + (h + 1) * half], result[:, columns])
+            first = work.tile([P, HALF], F32, name="first")
+            nc.vector.tensor_copy(first[:], flipped[piece][0][:])
+            nc.sync.dma_start(out[:, piece * PIECE : piece * PIECE + HALF], first[:])
+            second = work.tile([P, HALF], F32, name="second")
+            nc.scalar.copy(second[:], flipped[piece][1][:])
+            nc.scalar.dma_start(out[:, piece * PIECE + HALF : (piece + 1) * PIECE], second[:])

import math

import concourse.mybir as mybir
from concourse.masks import make_identity

BF16, F32, U16 = mybir.dt.bfloat16, mybir.dt.float32, mybir.dt.uint16
EXP = mybir.ActivationFunctionType.Exp
COPY = mybir.ActivationFunctionType.Copy
X = mybir.AxisListType.X

P = 128
TOKENS = 1024
KEYS = 512
N = 1024
PIECE = 512
PIECES = N // PIECE
KEY_BLOCKS = KEYS // P
QUERY_BLOCKS = PIECE // P
HALF = PIECE // 2
ONES = P
VALUE_COLUMNS = 144
WARM_UPS = 4

FLOPS = 2 * (2 * P * KEYS * N)


def tile_longcontextattention_kernel(tc, q, k, v, offs, out):
    nc = tc.nc
    with (
        tc.tile_pool(name="held", bufs=1) as held,
        tc.tile_pool(name="work", bufs=2) as work,
        tc.psum_pool(name="banks", bufs=8) as banks,
    ):
        offsets = held.tile([P, N // 16], U16, name="offsets")
        nc.sync.dma_start(offsets[:], offs)
        queries = held.tile([P, TOKENS], BF16, name="queries")
        nc.scalar.dma_start(queries[:], q)
        keys = held.tile([P, KEYS], BF16, name="keys")
        nc.sync.dma_start(keys[:], k)

        warm = held.tile([P, 1], F32, name="warm")
        nc.vector.memset(warm[:], 0.0)
        nc.scalar.activation(warm[:], warm[:], EXP)

        values = held.tile([P, KEY_BLOCKS, VALUE_COLUMNS], BF16, name="values")
        nc.gpsimd.dma_start(values[:, :, 0:P], v.rearrange("(b p) d -> p b d", p=P))
        nc.vector.memset(values[:, :, ONES:VALUE_COLUMNS], 1.0)

        identity = held.tile([P, P], F32, name="identity")
        make_identity(nc, identity[:])
        identity_bf16 = held.tile([P, P], BF16, name="identity_bf16")
        make_identity(nc, identity_bf16[:])

        zeros = held.tile([P, PIECE], BF16, name="zeros")
        nc.vector.memset(zeros[:], 0.0)
        for i in range(WARM_UPS):
            unused = banks.tile([P, PIECE], F32, name="unused", tag="bank")
            nc.tensor.matmul(unused[:], zeros[:, 0:P], zeros[:], start=True, stop=True)

        logits = [[] for piece in range(PIECES)]
        largest = [held.tile([P, PIECE], BF16, name=f"largest_{piece}") for piece in range(PIECES)]
        for piece in range(PIECES):
            piece_offsets = offsets[:, piece * (PIECE // 16) : (piece + 1) * (PIECE // 16)]
            for b in range(KEY_BLOCKS):
                product = banks.tile([P, PIECE], F32, name="product", tag="bank")
                nc.tensor.matmul(
                    product[:], keys[:, b * P : (b + 1) * P], queries[:].indirect(piece_offsets), start=True, stop=True
                )
                if b > 0:
                    so_far = logits[piece][0] if b == 1 else largest[piece]
                    nc.vector.tensor_max(largest[piece][:], product[:], so_far[:])
                logits[piece].append(held.tile([P, PIECE], F32, name=f"logits_{piece}_{b}"))
                nc.scalar.copy(logits[piece][b][:], product[:])

        top = []
        for piece in range(PIECES):
            flipped_largest = banks.tile([P, QUERY_BLOCKS, P], BF16, name="flipped_largest", tag="bank")
            for c in range(QUERY_BLOCKS):
                nc.tensor.transpose(flipped_largest[:, c, :], largest[piece][:, c * P : (c + 1) * P], identity_bf16[:])
            top.append(held.tile([P, QUERY_BLOCKS], BF16, name=f"top_{piece}"))
            with nc.allow_low_precision(reason="the maximum of bfloat16 numbers is one of them"):
                nc.vector.reduce_max(top[piece][:], flipped_largest[:], X)

        tops = []
        for piece in range(PIECES):
            tops.append(banks.tile([P, PIECE], BF16, name=f"tops_{piece}", tag="bank"))
            for c in range(QUERY_BLOCKS):
                nc.tensor.transpose(
                    tops[piece][:, c * P : (c + 1) * P], top[piece][:, c : c + 1].to_broadcast([P, P]), identity_bf16[:]
                )

        e = [[] for piece in range(PIECES)]
        for piece in range(PIECES):
            for b in range(KEY_BLOCKS):
                shifted = held.tile([P, PIECE], F32, name=f"shifted_{piece}_{b}")
                nc.vector.tensor_sub(shifted[:], logits[piece][b][:], tops[piece][:])
                e[piece].append(held.tile([P, PIECE], BF16, name=f"e_{piece}_{b}"))
                nc.scalar.activation(e[piece][b][:], shifted[:], EXP, scale=1.0 / math.sqrt(P))

        sums = []
        for piece in range(PIECES):
            sums.append([banks.tile([P, P + 1], F32, name=f"sums_{piece}_{c}", tag="bank") for c in range(QUERY_BLOCKS)])
            for b in range(KEY_BLOCKS):
                for c in range(QUERY_BLOCKS):
                    nc.tensor.matmul(
                        sums[piece][c][:],
                        e[piece][b][:, c * P : (c + 1) * P],
                        values[:, b, 0 : P + 1],
                        start=(b == 0),
                        stop=(b == KEY_BLOCKS - 1),
                    )

        flipped = []
        for piece in range(PIECES):
            inverse = work.tile([P, QUERY_BLOCKS], F32, name="inverse")
            for c in range(QUERY_BLOCKS):
                nc.vector.reciprocal(inverse[:, c : c + 1], sums[piece][c][:, ONES : ONES + 1])
            flipped.append([banks.tile([P, HALF], F32, name=f"flipped_{piece}_{h}", tag="bank") for h in range(2)])
            for c in range(QUERY_BLOCKS):
                attended = work.tile([P, P], F32, name="attended")
                if c % 2 == 0:
                    nc.vector.tensor_scalar_mul(attended[:], sums[piece][c][:, 0:P], inverse[:, c : c + 1])
                else:
                    nc.scalar.activation(attended[:], sums[piece][c][:, 0:P], COPY, scale=inverse[:, c : c + 1])
                h, place = divmod(c * P, HALF)
                nc.tensor.transpose(flipped[piece][h][:, place : place + P], attended[:], identity[:])

        for piece in range(PIECES):
            first = work.tile([P, HALF], F32, name="first")
            nc.vector.tensor_copy(first[:], flipped[piece][0][:])
            nc.sync.dma_start(out[:, piece * PIECE : piece * PIECE + HALF], first[:])
            second = work.tile([P, HALF], F32, name="second")
            nc.scalar.copy(second[:], flipped[piece][1][:])
            nc.scalar.dma_start(out[:, piece * PIECE + HALF : (piece + 1) * PIECE], second[:])
